import numpy as np
import ml_dtypes

BF16 = ml_dtypes.bfloat16


def bf(x):
    return np.asarray(x, np.float32).astype(BF16)


def f32(x):
    return np.asarray(x, np.float32)


def f64(x):
    return np.asarray(x).astype(np.float64)


def striped(idx):
    return np.tile(idx.reshape(-1, 16).T, (8, 1))


D, S, H, O, N = 128, 512, 512, 512, 256
SC = 0.05


def silu(v):
    return v / (1.0 + np.exp(-v))


def setup_inputs():
    return {
        "table": bf(np.random.standard_normal((D, S))),
        "v0": bf(SC * np.random.standard_normal((D, H))),
        "g0": f32(1.0 + 0.1 * np.random.standard_normal((H, 1))),
        "b0": f32(0.1 * np.random.standard_normal((H, 1))),
        "v1": bf(SC * np.random.standard_normal((H, H))),
        "g1": f32(1.0 + 0.1 * np.random.standard_normal((H, 1))),
        "b1": f32(0.1 * np.random.standard_normal((H, 1))),
        "wf": bf(2.0 * SC * np.random.standard_normal((H, O))),
        "bo": f32(0.1 * np.random.standard_normal((O, 1))),
        "offs": striped(np.random.permutation(S)[:N]),
    }


def reference(table, v0, g0, b0, v1, g1, b1, wf, bo, offs):
    idx = offs[:16].T.reshape(-1)
    s0 = f64(g0) / np.sqrt(np.sum(np.square(f64(v0)), axis=0))[:, None]
    s1 = f64(g1) / np.sqrt(np.sum(np.square(f64(v1)), axis=0))[:, None]
    h1 = silu(s0 * (f64(v0).T @ f64(table)[:, idx]) + f64(b0))
    h2 = silu(s1 * (f64(v1).T @ h1) + f64(b1))
    return f64(wf).T @ h2 + f64(bo)

@@ -1,0 +1,111 @@
+import concourse.mybir as mybir
+from concourse.masks import make_identity
+
+P = 128
+D, S, H, O, N = 128, 512, 512, 512, 256
+BLOCKS = H // P
+assert D == P and H == O
+
+FLOPS = 2 * N * (D * H + H * H + H * O)
+BYTES = 2 * (D * N + D * H + H * H + H * O) + 4 * (4 * H + O) + 2 * P * (N // 16) + 4 * O * N
+
+BF16, F32, U16 = mybir.dt.bfloat16, mybir.dt.float32, mybir.dt.uint16
+MULT, POW = mybir.AluOpType.mult, mybir.AluOpType.pow
+SILU = mybir.ActivationFunctionType.Silu
+IDENTITY = mybir.ActivationFunctionType.Identity
+
+
+def tile_hypernetfullyconnectedflexilayersizearch_kernel(
+    tc, table, v0, g0, b0, v1, g1, b1, wf, bo, offs, out
+):
+    nc = tc.nc
+    with (
+        tc.tile_pool(name="held", bufs=1) as held,
+        tc.psum_pool(name="psum_acc", bufs=6) as psum_acc,
+        tc.psum_pool(name="psum_gram", bufs=2) as psum_gram,
+    ):
+        offsets = held.tile([P, N // 16], U16, name="offsets")
+        nc.sync.dma_start(offsets[:], offs)
+        v0_sb = held.tile([P, H], BF16, name="v0_sb")
+        nc.sync.dma_start(v0_sb[:], v0)
+        table_sb = held.tile([P, S], BF16, name="table_sb")
+        nc.scalar.dma_start(table_sb[:], table)
+
+        def load_vector(queue, vector, name):
+            columns = held.tile([P, BLOCKS], F32, name=name)
+            queue.dma_start(columns[:], vector.rearrange("(p c) one -> p (c one)", c=BLOCKS))
+            return columns
+
+        g0_sb = load_vector(nc.sync, g0, "g0_sb")
+        b0_sb = load_vector(nc.scalar, b0, "b0_sb")
+        v1_sb = held.tile([P, BLOCKS, H], BF16, name="v1_sb")
+        nc.sync.dma_start(v1_sb[:], v1.rearrange("(p kb) m -> p kb m", kb=BLOCKS))
+        wf_sb = held.tile([P, BLOCKS, O], BF16, name="wf_sb")
+        nc.sync.dma_start(wf_sb[:], wf.rearrange("(p kb) m -> p kb m", kb=BLOCKS))
+        g1_sb = load_vector(nc.gpsimd, g1, "g1_sb")
+        b1_sb = load_vector(nc.gpsimd, b1, "b1_sb")
+        bo_sb = load_vector(nc.gpsimd, bo, "bo_sb")
+
+        v0_blocks = [v0_sb[:].rearrange("k (p c) -> k c p", c=BLOCKS)]
+        v1_view = v1_sb[:].rearrange("k kb (p c) -> k kb c p", c=BLOCKS)
+        v1_blocks = [v1_view[:, kb] for kb in range(BLOCKS)]
+        wf_view = wf_sb[:].rearrange("k kb (p c) -> k kb c p", c=BLOCKS)
+        wf_blocks = [wf_view[:, kb] for kb in range(BLOCKS)]
+        out_blocks = out.rearrange("(p c) j -> p c j", c=BLOCKS)
+
+        identity = held.tile([P, P], F32, name="identity")
+        make_identity(nc, identity[:])
+        minus_half = held.tile([P, BLOCKS], F32, name="minus_half")
+        nc.vector.memset(minus_half[:], -0.5)
+
+        def weight_norm_scale(weight_blocks, gain, name):
+            gram = psum_gram.tile([P, BLOCKS, P], F32, name="gram")
+            last = len(weight_blocks) - 1
+            for c in range(BLOCKS):
+                for kb, block in enumerate(weight_blocks):
+                    nc.tensor.matmul(
+                        gram[:, c, :], block[:, c, :], block[:, c, :], start=kb == 0, stop=kb == last
+                    )
+            diagonal = held.tile([P, BLOCKS, P], F32, name=name + "_diagonal")
+            nc.vector.tensor_tensor(
+                diagonal[:], gram[:], identity[:].unsqueeze(1).to_broadcast([P, BLOCKS, P]), MULT
+            )
+            sum_squares = held.tile([P, BLOCKS], F32, name=name + "_sum_squares")
+            nc.vector.reduce_sum(sum_squares[:], diagonal[:], axis=mybir.AxisListType.X)
+            inverse_norm = held.tile([P, BLOCKS], F32, name=name + "_inverse_norm")
+            nc.gpsimd.tensor_tensor(inverse_norm[:], sum_squares[:], minus_half[:], POW)
+            scale = held.tile([P, BLOCKS], F32, name=name)
+            nc.gpsimd.tensor_tensor(scale[:], inverse_norm[:], gain[:], MULT)
+            return scale
+
+        def project(weight_blocks, moving_blocks):
+            accs = [psum_acc.tile([P, N], F32, name=f"acc{c}", tag="acc") for c in range(BLOCKS)]
+            last = len(weight_blocks) - 1
+            for kb, (block, moving) in enumerate(zip(weight_blocks, moving_blocks)):
+                for c in range(BLOCKS):
+                    nc.tensor.matmul(accs[c][:], block[:, c, :], moving, start=kb == 0, stop=kb == last)
+            return accs
+
+        def silu_blocks(accs, scale, bias, name):
+            hidden = [held.tile([P, N], BF16, name=f"{name}_{c}") for c in range(BLOCKS)]
+            for c in range(BLOCKS):
+                nc.scalar.activation(
+                    hidden[c][:], accs[c][:], SILU, bias=bias[:, c : c + 1], scale=scale[:, c : c + 1]
+                )
+            return [h[:] for h in hidden]
+
+        v0_packed = held.tile([P, BLOCKS, P], BF16, name="v0_packed")
+        nc.vector.tensor_copy(v0_packed[:], v0_blocks[0])
+        s0 = weight_norm_scale(v0_blocks, g0_sb, "s0")
+        h1 = silu_blocks(project([v0_packed[:]], [table_sb[:].indirect(offsets[:])]), s0, b0_sb, "h1")
+        s1 = weight_norm_scale(v1_blocks, g1_sb, "s1")
+        h2 = silu_blocks(project(v1_blocks, h1), s1, b1_sb, "h2")
+        accs = project(wf_blocks, h2)
+        for c in range(BLOCKS):
+            result = held.tile([P, N], F32, name=f"result{c}")
+            if c % 2 == 0:
+                nc.vector.tensor_scalar_add(result[:], accs[c][:], bo_sb[:, c : c + 1])
+                nc.sync.dma_start(out_blocks[:, c, :], result[:])
+            else:
+                nc.scalar.activation(result[:], accs[c][:], IDENTITY, bias=bo_sb[:, c : c + 1])
+                nc.scalar.dma_start(out_blocks[:, c, :], result[:])

@@ -5,6 +5,8 @@ P = 128
 D, S, H, O, N = 128, 512, 512, 512, 256
 BLOCKS = H // P
 assert D == P and H == O
+WARM_COLUMNS = 512
+WARM_MATMULS = 3
 
 FLOPS = 2 * N * (D * H + H * H + H * O)
 BYTES = 2 * (D * N + D * H + H * H + H * O) + 4 * (4 * H + O) + 2 * P * (N // 16) + 4 * O * N
@@ -21,15 +23,29 @@ def tile_hypernetfullyconnectedflexilayersizearch_kernel(
     nc = tc.nc
     with (
         tc.tile_pool(name="held", bufs=1) as held,
+        tc.tile_pool(name="scratch", bufs=2) as scratch,
         tc.psum_pool(name="psum_acc", bufs=6) as psum_acc,
         tc.psum_pool(name="psum_gram", bufs=2) as psum_gram,
     ):
-        offsets = held.tile([P, N // 16], U16, name="offsets")
-        nc.sync.dma_start(offsets[:], offs)
+        warm_src = held.tile([P, WARM_COLUMNS], BF16, name="warm_src")
+        nc.gpsimd.memset(warm_src[:], 0.0)
+        identity = held.tile([P, P], F32, name="identity")
+        make_identity(nc, identity[:])
+        minus_half = held.tile([P, BLOCKS], F32, name="minus_half")
+        nc.vector.memset(minus_half[:], -0.5)
+
+        warm_acc = psum_gram.tile([P, WARM_COLUMNS], F32, name="warm_acc", tag="gram")
+        for i in range(WARM_MATMULS):
+            nc.tensor.matmul(warm_acc[:], warm_src[:, 0:P], warm_src[:], start=True, stop=True)
+        warm_silu = held.tile([P, 1], F32, name="warm_silu")
+        nc.scalar.activation(warm_silu[:], minus_half[:, 0:1], SILU)
+
         v0_sb = held.tile([P, H], BF16, name="v0_sb")
         nc.sync.dma_start(v0_sb[:], v0)
         table_sb = held.tile([P, S], BF16, name="table_sb")
-        nc.scalar.dma_start(table_sb[:], table)
+        nc.sync.dma_start(table_sb[:], table)
+        offsets = held.tile([P, N // 16], U16, name="offsets")
+        nc.sync.dma_start(offsets[:], offs)
 
         def load_vector(queue, vector, name):
             columns = held.tile([P, BLOCKS], F32, name=name)
@@ -37,14 +53,14 @@ def tile_hypernetfullyconnectedflexilayersizearch_kernel(
             return columns
 
         g0_sb = load_vector(nc.sync, g0, "g0_sb")
-        b0_sb = load_vector(nc.scalar, b0, "b0_sb")
+        b0_sb = load_vector(nc.sync, b0, "b0_sb")
         v1_sb = held.tile([P, BLOCKS, H], BF16, name="v1_sb")
         nc.sync.dma_start(v1_sb[:], v1.rearrange("(p kb) m -> p kb m", kb=BLOCKS))
+        g1_sb = load_vector(nc.sync, g1, "g1_sb")
+        b1_sb = load_vector(nc.sync, b1, "b1_sb")
         wf_sb = held.tile([P, BLOCKS, O], BF16, name="wf_sb")
         nc.sync.dma_start(wf_sb[:], wf.rearrange("(p kb) m -> p kb m", kb=BLOCKS))
-        g1_sb = load_vector(nc.gpsimd, g1, "g1_sb")
-        b1_sb = load_vector(nc.gpsimd, b1, "b1_sb")
-        bo_sb = load_vector(nc.gpsimd, bo, "bo_sb")
+        bo_sb = load_vector(nc.sync, bo, "bo_sb")
 
         v0_blocks = [v0_sb[:].rearrange("k (p c) -> k c p", c=BLOCKS)]
         v1_view = v1_sb[:].rearrange("k kb (p c) -> k kb c p", c=BLOCKS)
@@ -53,29 +69,30 @@ def tile_hypernetfullyconnectedflexilayersizearch_kernel(
         wf_blocks = [wf_view[:, kb] for kb in range(BLOCKS)]
         out_blocks = out.rearrange("(p c) j -> p c j", c=BLOCKS)
 
-        identity = held.tile([P, P], F32, name="identity")
-        make_identity(nc, identity[:])
-        minus_half = held.tile([P, BLOCKS], F32, name="minus_half")
-        nc.vector.memset(minus_half[:], -0.5)
-
-        def weight_norm_scale(weight_blocks, gain, name):
-            gram = psum_gram.tile([P, BLOCKS, P], F32, name="gram")
-            last = len(weight_blocks) - 1
-            for c in range(BLOCKS):
-                for kb, block in enumerate(weight_blocks):
-                    nc.tensor.matmul(
-                        gram[:, c, :], block[:, c, :], block[:, c, :], start=kb == 0, stop=kb == last
-                    )
-            diagonal = held.tile([P, BLOCKS, P], F32, name=name + "_diagonal")
-            nc.vector.tensor_tensor(
-                diagonal[:], gram[:], identity[:].unsqueeze(1).to_broadcast([P, BLOCKS, P]), MULT
-            )
+        def weight_norm_scale(weight_blocks, gain, blocks_at_a_time, name):
             sum_squares = held.tile([P, BLOCKS], F32, name=name + "_sum_squares")
-            nc.vector.reduce_sum(sum_squares[:], diagonal[:], axis=mybir.AxisListType.X)
             inverse_norm = held.tile([P, BLOCKS], F32, name=name + "_inverse_norm")
-            nc.gpsimd.tensor_tensor(inverse_norm[:], sum_squares[:], minus_half[:], POW)
             scale = held.tile([P, BLOCKS], F32, name=name)
-            nc.gpsimd.tensor_tensor(scale[:], inverse_norm[:], gain[:], MULT)
+            last = len(weight_blocks) - 1
+            pieces = [range(first, first + blocks_at_a_time) for first in range(0, BLOCKS, blocks_at_a_time)]
+            for piece in pieces:
+                gram = psum_gram.tile([P, blocks_at_a_time, P], F32, name="gram", tag="gram")
+                for i, c in enumerate(piece):
+                    for kb, block in enumerate(weight_blocks):
+                        nc.tensor.matmul(
+                            gram[:, i, :], block[:, c, :], block[:, c, :], start=kb == 0, stop=kb == last
+                        )
+                for i, c in enumerate(piece):
+                    diagonal = scratch.tile([P, P], F32, name="diagonal")
+                    nc.vector.scalar_tensor_tensor(
+                        diagonal[:], gram[:, i, :], 1.0, identity[:], MULT, MULT, accum_out=sum_squares[:, c : c + 1]
+                    )
+            for piece in pieces:
+                columns = slice(piece[0], piece[0] + blocks_at_a_time)
+                nc.gpsimd.tensor_tensor(
+                    inverse_norm[:, columns], sum_squares[:, columns], minus_half[:, 0:blocks_at_a_time], POW
+                )
+                nc.vector.tensor_tensor(scale[:, columns], inverse_norm[:, columns], gain[:, columns], MULT)
             return scale
 
         def project(weight_blocks, moving_blocks):
@@ -94,11 +111,11 @@ def tile_hypernetfullyconnectedflexilayersizearch_kernel(
                 )
             return [h[:] for h in hidden]
 
+        s0 = weight_norm_scale(v0_blocks, g0_sb, BLOCKS // 2, "s0")
         v0_packed = held.tile([P, BLOCKS, P], BF16, name="v0_packed")
-        nc.vector.tensor_copy(v0_packed[:], v0_blocks[0])
-        s0 = weight_norm_scale(v0_blocks, g0_sb, "s0")
+        nc.scalar.copy(v0_packed[:], v0_blocks[0])
         h1 = silu_blocks(project([v0_packed[:]], [table_sb[:].indirect(offsets[:])]), s0, b0_sb, "h1")
-        s1 = weight_norm_scale(v1_blocks, g1_sb, "s1")
+        s1 = weight_norm_scale(v1_blocks, g1_sb, BLOCKS // 2, "s1")
         h2 = silu_blocks(project(v1_blocks, h1), s1, b1_sb, "h2")
         accs = project(wf_blocks, h2)
         for c in range(BLOCKS):

@@ -49,25 +49,26 @@ def tile_hypernetfullyconnectedflexilayersizearch_kernel(
 
         def load_vector(queue, vector, name):
             columns = held.tile([P, BLOCKS], F32, name=name)
-            queue.dma_start(columns[:], vector.rearrange("(p c) one -> p (c one)", c=BLOCKS))
+            with nc.allow_non_contiguous_dma(reason="512 floats, one to a partition and block"):
+                queue.dma_start(columns[:], vector.rearrange("(c p) one -> p (c one)", c=BLOCKS))
             return columns
 
         g0_sb = load_vector(nc.sync, g0, "g0_sb")
         b0_sb = load_vector(nc.sync, b0, "b0_sb")
         v1_sb = held.tile([P, BLOCKS, H], BF16, name="v1_sb")
-        nc.sync.dma_start(v1_sb[:], v1.rearrange("(p kb) m -> p kb m", kb=BLOCKS))
+        nc.sync.dma_start(v1_sb[:], v1.rearrange("(kb p) m -> p kb m", kb=BLOCKS))
         g1_sb = load_vector(nc.sync, g1, "g1_sb")
         b1_sb = load_vector(nc.sync, b1, "b1_sb")
         wf_sb = held.tile([P, BLOCKS, O], BF16, name="wf_sb")
-        nc.sync.dma_start(wf_sb[:], wf.rearrange("(p kb) m -> p kb m", kb=BLOCKS))
+        nc.sync.dma_start(wf_sb[:], wf.rearrange("(kb p) m -> p kb m", kb=BLOCKS))
         bo_sb = load_vector(nc.sync, bo, "bo_sb")
 
-        v0_blocks = [v0_sb[:].rearrange("k (p c) -> k c p", c=BLOCKS)]
-        v1_view = v1_sb[:].rearrange("k kb (p c) -> k kb c p", c=BLOCKS)
+        v0_blocks = [v0_sb[:].rearrange("k (c p) -> k c p", c=BLOCKS)]
+        v1_view = v1_sb[:].rearrange("k kb (c p) -> k kb c p", c=BLOCKS)
         v1_blocks = [v1_view[:, kb] for kb in range(BLOCKS)]
-        wf_view = wf_sb[:].rearrange("k kb (p c) -> k kb c p", c=BLOCKS)
+        wf_view = wf_sb[:].rearrange("k kb (c p) -> k kb c p", c=BLOCKS)
         wf_blocks = [wf_view[:, kb] for kb in range(BLOCKS)]
-        out_blocks = out.rearrange("(p c) j -> p c j", c=BLOCKS)
+        out_blocks = out.rearrange("(c p) j -> p c j", c=BLOCKS)
 
         def weight_norm_scale(weight_blocks, gain, blocks_at_a_time, name):
             sum_squares = held.tile([P, BLOCKS], F32, name=name + "_sum_squares")
@@ -112,9 +113,7 @@ def tile_hypernetfullyconnectedflexilayersizearch_kernel(
             return [h[:] for h in hidden]
 
         s0 = weight_norm_scale(v0_blocks, g0_sb, BLOCKS // 2, "s0")
-        v0_packed = held.tile([P, BLOCKS, P], BF16, name="v0_packed")
-        nc.scalar.copy(v0_packed[:], v0_blocks[0])
-        h1 = silu_blocks(project([v0_packed[:]], [table_sb[:].indirect(offsets[:])]), s0, b0_sb, "h1")
+        h1 = silu_blocks(project(v0_blocks, [table_sb[:].indirect(offsets[:])]), s0, b0_sb, "h1")
         s1 = weight_norm_scale(v1_blocks, g1_sb, BLOCKS // 2, "s1")
         h2 = silu_blocks(project(v1_blocks, h1), s1, b1_sb, "h2")
         accs = project(wf_blocks, h2)

@@ -5,8 +5,7 @@ P = 128
 D, S, H, O, N = 128, 512, 512, 512, 256
 BLOCKS = H // P
 assert D == P and H == O
-WARM_COLUMNS = 512
-WARM_MATMULS = 3
+WARM_MATMULS = 12
 
 FLOPS = 2 * N * (D * H + H * H + H * O)
 BYTES = 2 * (D * N + D * H + H * H + H * O) + 4 * (4 * H + O) + 2 * P * (N // 16) + 4 * O * N
@@ -27,16 +26,16 @@ def tile_hypernetfullyconnectedflexilayersizearch_kernel(
         tc.psum_pool(name="psum_acc", bufs=6) as psum_acc,
         tc.psum_pool(name="psum_gram", bufs=2) as psum_gram,
     ):
-        warm_src = held.tile([P, WARM_COLUMNS], BF16, name="warm_src")
+        warm_src = held.tile([P, P], BF16, name="warm_src")
         nc.gpsimd.memset(warm_src[:], 0.0)
         identity = held.tile([P, P], F32, name="identity")
         make_identity(nc, identity[:])
         minus_half = held.tile([P, BLOCKS], F32, name="minus_half")
         nc.vector.memset(minus_half[:], -0.5)
 
-        warm_acc = psum_gram.tile([P, WARM_COLUMNS], F32, name="warm_acc", tag="gram")
+        warm_acc = psum_gram.tile([P, P], F32, name="warm_acc", tag="gram")
         for i in range(WARM_MATMULS):
-            nc.tensor.matmul(warm_acc[:], warm_src[:, 0:P], warm_src[:], start=True, stop=True)
+            nc.tensor.matmul(warm_acc[:], warm_src[:], warm_src[:], start=True, stop=True)
         warm_silu = held.tile([P, 1], F32, name="warm_silu")
         nc.scalar.activation(warm_silu[:], minus_half[:, 0:1], SILU)
 
@@ -53,15 +52,15 @@ def tile_hypernetfullyconnectedflexilayersizearch_kernel(
                 queue.dma_start(columns[:], vector.rearrange("(c p) one -> p (c one)", c=BLOCKS))
             return columns
 
-        g0_sb = load_vector(nc.sync, g0, "g0_sb")
-        b0_sb = load_vector(nc.sync, b0, "b0_sb")
+        g0_sb = load_vector(nc.scalar, g0, "g0_sb")
+        b0_sb = load_vector(nc.scalar, b0, "b0_sb")
         v1_sb = held.tile([P, BLOCKS, H], BF16, name="v1_sb")
         nc.sync.dma_start(v1_sb[:], v1.rearrange("(kb p) m -> p kb m", kb=BLOCKS))
-        g1_sb = load_vector(nc.sync, g1, "g1_sb")
-        b1_sb = load_vector(nc.sync, b1, "b1_sb")
+        g1_sb = load_vector(nc.scalar, g1, "g1_sb")
+        b1_sb = load_vector(nc.scalar, b1, "b1_sb")
         wf_sb = held.tile([P, BLOCKS, O], BF16, name="wf_sb")
         nc.sync.dma_start(wf_sb[:], wf.rearrange("(kb p) m -> p kb m", kb=BLOCKS))
-        bo_sb = load_vector(nc.sync, bo, "bo_sb")
+        bo_sb = load_vector(nc.scalar, bo, "bo_sb")
 
         v0_blocks = [v0_sb[:].rearrange("k (c p) -> k c p", c=BLOCKS)]
         v1_view = v1_sb[:].rearrange("k kb (c p) -> k kb c p", c=BLOCKS)
@@ -98,10 +97,19 @@ def tile_hypernetfullyconnectedflexilayersizearch_kernel(
 
         def project(weight_blocks, moving_blocks):
             accs = [psum_acc.tile([P, N], F32, name=f"acc{c}", tag="acc") for c in range(BLOCKS)]
-            last = len(weight_blocks) - 1
-            for kb, (block, moving) in enumerate(zip(weight_blocks, moving_blocks)):
+            count = len(weight_blocks)
+
+            def accumulate(c, kb):
+                nc.tensor.matmul(
+                    accs[c][:], weight_blocks[kb][:, c, :], moving_blocks[kb], start=kb == 0, stop=kb == count - 1
+                )
+
+            for kb in range(count // 2):
                 for c in range(BLOCKS):
-                    nc.tensor.matmul(accs[c][:], block[:, c, :], moving, start=kb == 0, stop=kb == last)
+                    accumulate(c, kb)
+            for c in range(BLOCKS):
+                for kb in range(count // 2, count):
+                    accumulate(c, kb)
             return accs
 
         def silu_blocks(accs, scale, bias, name):

@@ -5,7 +5,7 @@ P = 128
 D, S, H, O, N = 128, 512, 512, 512, 256
 BLOCKS = H // P
 assert D == P and H == O
-WARM_MATMULS = 12
+WARM_MATMULS = 16
 
 FLOPS = 2 * N * (D * H + H * H + H * O)
 BYTES = 2 * (D * N + D * H + H * H + H * O) + 4 * (4 * H + O) + 2 * P * (N // 16) + 4 * O * N
@@ -52,15 +52,15 @@ def tile_hypernetfullyconnectedflexilayersizearch_kernel(
                 queue.dma_start(columns[:], vector.rearrange("(c p) one -> p (c one)", c=BLOCKS))
             return columns
 
-        g0_sb = load_vector(nc.scalar, g0, "g0_sb")
-        b0_sb = load_vector(nc.scalar, b0, "b0_sb")
+        g0_sb = load_vector(nc.sync, g0, "g0_sb")
+        b0_sb = load_vector(nc.sync, b0, "b0_sb")
         v1_sb = held.tile([P, BLOCKS, H], BF16, name="v1_sb")
         nc.sync.dma_start(v1_sb[:], v1.rearrange("(kb p) m -> p kb m", kb=BLOCKS))
-        g1_sb = load_vector(nc.scalar, g1, "g1_sb")
-        b1_sb = load_vector(nc.scalar, b1, "b1_sb")
+        g1_sb = load_vector(nc.sync, g1, "g1_sb")
+        b1_sb = load_vector(nc.sync, b1, "b1_sb")
         wf_sb = held.tile([P, BLOCKS, O], BF16, name="wf_sb")
         nc.sync.dma_start(wf_sb[:], wf.rearrange("(kb p) m -> p kb m", kb=BLOCKS))
-        bo_sb = load_vector(nc.scalar, bo, "bo_sb")
+        bo_sb = load_vector(nc.sync, bo, "bo_sb")
 
         v0_blocks = [v0_sb[:].rearrange("k (c p) -> k c p", c=BLOCKS)]
         v1_view = v1_sb[:].rearrange("k kb (c p) -> k kb c p", c=BLOCKS)

@@ -52,10 +52,10 @@ def tile_hypernetfullyconnectedflexilayersizearch_kernel(
                 queue.dma_start(columns[:], vector.rearrange("(c p) one -> p (c one)", c=BLOCKS))
             return columns
 
-        g0_sb = load_vector(nc.sync, g0, "g0_sb")
-        b0_sb = load_vector(nc.sync, b0, "b0_sb")
         v1_sb = held.tile([P, BLOCKS, H], BF16, name="v1_sb")
         nc.sync.dma_start(v1_sb[:], v1.rearrange("(kb p) m -> p kb m", kb=BLOCKS))
+        g0_sb = load_vector(nc.sync, g0, "g0_sb")
+        b0_sb = load_vector(nc.sync, b0, "b0_sb")
         g1_sb = load_vector(nc.sync, g1, "g1_sb")
         b1_sb = load_vector(nc.sync, b1, "b1_sb")
         wf_sb = held.tile([P, BLOCKS, O], BF16, name="wf_sb")

@@ -23,8 +23,7 @@ def tile_hypernetfullyconnectedflexilayersizearch_kernel(
     with (
         tc.tile_pool(name="held", bufs=1) as held,
         tc.tile_pool(name="scratch", bufs=2) as scratch,
-        tc.psum_pool(name="psum_acc", bufs=6) as psum_acc,
-        tc.psum_pool(name="psum_gram", bufs=2) as psum_gram,
+        tc.psum_pool(name="psum", bufs=8) as psum,
     ):
         warm_src = held.tile([P, P], BF16, name="warm_src")
         nc.gpsimd.memset(warm_src[:], 0.0)
@@ -33,7 +32,7 @@ def tile_hypernetfullyconnectedflexilayersizearch_kernel(
         minus_half = held.tile([P, BLOCKS], F32, name="minus_half")
         nc.vector.memset(minus_half[:], -0.5)
 
-        warm_acc = psum_gram.tile([P, P], F32, name="warm_acc", tag="gram")
+        warm_acc = psum.tile([P, P], F32, name="warm_acc", tag="bank")
         for i in range(WARM_MATMULS):
             nc.tensor.matmul(warm_acc[:], warm_src[:], warm_src[:], start=True, stop=True)
         warm_silu = held.tile([P, 1], F32, name="warm_silu")
@@ -76,7 +75,7 @@ def tile_hypernetfullyconnectedflexilayersizearch_kernel(
             last = len(weight_blocks) - 1
             pieces = [range(first, first + blocks_at_a_time) for first in range(0, BLOCKS, blocks_at_a_time)]
             for piece in pieces:
-                gram = psum_gram.tile([P, blocks_at_a_time, P], F32, name="gram", tag="gram")
+                gram = psum.tile([P, blocks_at_a_time, P], F32, name="gram", tag="bank")
                 for i, c in enumerate(piece):
                     for kb, block in enumerate(weight_blocks):
                         nc.tensor.matmul(
@@ -95,21 +94,29 @@ def tile_hypernetfullyconnectedflexilayersizearch_kernel(
                 nc.vector.tensor_tensor(scale[:, columns], inverse_norm[:, columns], gain[:, columns], MULT)
             return scale
 
-        def project(weight_blocks, moving_blocks):
-            accs = [psum_acc.tile([P, N], F32, name=f"acc{c}", tag="acc") for c in range(BLOCKS)]
+        def project(weight_blocks, moving_blocks, tiles):
+            accs = [
+                psum.tile([P, columns.stop - columns.start], F32, name=f"acc{t}", tag="bank")
+                for t, (c, columns) in enumerate(tiles)
+            ]
             count = len(weight_blocks)
 
-            def accumulate(c, kb):
+            def accumulate(t, kb):
+                c, columns = tiles[t]
                 nc.tensor.matmul(
-                    accs[c][:], weight_blocks[kb][:, c, :], moving_blocks[kb], start=kb == 0, stop=kb == count - 1
+                    accs[t][:],
+                    weight_blocks[kb][:, c, :],
+                    moving_blocks[kb][:, columns],
+                    start=kb == 0,
+                    stop=kb == count - 1,
                 )
 
             for kb in range(count // 2):
-                for c in range(BLOCKS):
-                    accumulate(c, kb)
-            for c in range(BLOCKS):
+                for t in range(len(tiles)):
+                    accumulate(t, kb)
+            for t in range(len(tiles)):
                 for kb in range(count // 2, count):
-                    accumulate(c, kb)
+                    accumulate(t, kb)
             return accs
 
         def silu_blocks(accs, scale, bias, name):
@@ -120,16 +127,23 @@ def tile_hypernetfullyconnectedflexilayersizearch_kernel(
                 )
             return [h[:] for h in hidden]
 
+        whole_tiles = [(c, slice(0, N)) for c in range(BLOCKS)]
+
         s0 = weight_norm_scale(v0_blocks, g0_sb, BLOCKS // 2, "s0")
-        h1 = silu_blocks(project(v0_blocks, [table_sb[:].indirect(offsets[:])]), s0, b0_sb, "h1")
-        s1 = weight_norm_scale(v1_blocks, g1_sb, BLOCKS // 2, "s1")
-        h2 = silu_blocks(project(v1_blocks, h1), s1, b1_sb, "h2")
-        accs = project(wf_blocks, h2)
+        looked_up = table_sb[:].indirect(offsets[:])
+        accs = [psum.tile([P, N], F32, name=f"picked{c}", tag="bank") for c in range(BLOCKS)]
         for c in range(BLOCKS):
-            result = held.tile([P, N], F32, name=f"result{c}")
-            if c % 2 == 0:
-                nc.vector.tensor_scalar_add(result[:], accs[c][:], bo_sb[:, c : c + 1])
-                nc.sync.dma_start(out_blocks[:, c, :], result[:])
+            nc.tensor.matmul(accs[c][:], v0_blocks[0][:, c, :], looked_up, start=True, stop=True)
+        h1 = silu_blocks(accs, s0, b0_sb, "h1")
+        s1 = weight_norm_scale(v1_blocks, g1_sb, BLOCKS // 2, "s1")
+        h2 = silu_blocks(project(v1_blocks, h1, whole_tiles), s1, b1_sb, "h2")
+        out_tiles = whole_tiles[:-1] + [(BLOCKS - 1, slice(0, N // 2)), (BLOCKS - 1, slice(N // 2, N))]
+        accs = project(wf_blocks, h2, out_tiles)
+        for t, (c, columns) in enumerate(out_tiles):
+            result = held.tile([P, columns.stop - columns.start], F32, name=f"result{t}")
+            if t % 2 == 0:
+                nc.vector.tensor_scalar_add(result[:], accs[t][:], bo_sb[:, c : c + 1])
+                nc.sync.dma_start(out_blocks[:, c, columns], result[:])
             else:
-                nc.scalar.activation(result[:], accs[c][:], IDENTITY, bias=bo_sb[:, c : c + 1])
-                nc.scalar.dma_start(out_blocks[:, c, :], result[:])
+                nc.scalar.activation(result[:], accs[t][:], IDENTITY, bias=bo_sb[:, c : c + 1])
+                nc.scalar.dma_start(out_blocks[:, c, columns], result[:])

@@ -94,56 +94,47 @@ def tile_hypernetfullyconnectedflexilayersizearch_kernel(
                 nc.vector.tensor_tensor(scale[:, columns], inverse_norm[:, columns], gain[:, columns], MULT)
             return scale
 
-        def project(weight_blocks, moving_blocks, tiles):
-            accs = [
-                psum.tile([P, columns.stop - columns.start], F32, name=f"acc{t}", tag="bank")
-                for t, (c, columns) in enumerate(tiles)
-            ]
-            count = len(weight_blocks)
-
-            def accumulate(t, kb):
-                c, columns = tiles[t]
+        def project(weight_blocks, moving_blocks, block_by_block):
+            width = moving_blocks[0].shape[1]
+            accs = [psum.tile([P, width], F32, name=f"acc{c}", tag="bank") for c in range(BLOCKS)]
+            if block_by_block:
+                order = [(c, kb) for kb in range(BLOCKS) for c in range(BLOCKS)]
+            else:
+                order = [(c, kb) for c in range(BLOCKS) for kb in range(BLOCKS)]
+            for c, kb in order:
                 nc.tensor.matmul(
-                    accs[t][:],
-                    weight_blocks[kb][:, c, :],
-                    moving_blocks[kb][:, columns],
-                    start=kb == 0,
-                    stop=kb == count - 1,
+                    accs[c][:], weight_blocks[kb][:, c, :], moving_blocks[kb], start=kb == 0, stop=kb == BLOCKS - 1
                 )
-
-            for kb in range(count // 2):
-                for t in range(len(tiles)):
-                    accumulate(t, kb)
-            for t in range(len(tiles)):
-                for kb in range(count // 2, count):
-                    accumulate(t, kb)
             return accs
 
         def silu_blocks(accs, scale, bias, name):
-            hidden = [held.tile([P, N], BF16, name=f"{name}_{c}") for c in range(BLOCKS)]
+            width = accs[0][:].shape[1]
+            hidden = [held.tile([P, width], BF16, name=f"{name}_{c}") for c in range(BLOCKS)]
             for c in range(BLOCKS):
                 nc.scalar.activation(
                     hidden[c][:], accs[c][:], SILU, bias=bias[:, c : c + 1], scale=scale[:, c : c + 1]
                 )
             return [h[:] for h in hidden]
 
-        whole_tiles = [(c, slice(0, N)) for c in range(BLOCKS)]
-
         s0 = weight_norm_scale(v0_blocks, g0_sb, BLOCKS // 2, "s0")
         looked_up = table_sb[:].indirect(offsets[:])
-        accs = [psum.tile([P, N], F32, name=f"picked{c}", tag="bank") for c in range(BLOCKS)]
+        picked = [psum.tile([P, N], F32, name=f"picked{c}", tag="bank") for c in range(BLOCKS)]
         for c in range(BLOCKS):
-            nc.tensor.matmul(accs[c][:], v0_blocks[0][:, c, :], looked_up, start=True, stop=True)
-        h1 = silu_blocks(accs, s0, b0_sb, "h1")
+            nc.tensor.matmul(picked[c][:], v0_blocks[0][:, c, :], looked_up, start=True, stop=True)
+        h1 = silu_blocks(picked, s0, b0_sb, "h1")
+
+        halves = [slice(0, N // 2), slice(N // 2, N)]
         s1 = weight_norm_scale(v1_blocks, g1_sb, BLOCKS // 2, "s1")
-        h2 = silu_blocks(project(v1_blocks, h1, whole_tiles), s1, b1_sb, "h2")
-        out_tiles = whole_tiles[:-1] + [(BLOCKS - 1, slice(0, N // 2)), (BLOCKS - 1, slice(N // 2, N))]
-        accs = project(wf_blocks, h2, out_tiles)
-        for t, (c, columns) in enumerate(out_tiles):
-            result = held.tile([P, columns.stop - columns.start], F32, name=f"result{t}")
-            if t % 2 == 0:
-                nc.vector.tensor_scalar_add(result[:], accs[t][:], bo_sb[:, c : c + 1])
+        h2 = []
+        for half, columns in enumerate(halves):
+            accs = project(v1_blocks, [h[:, columns] for h in h1], block_by_block=half == 0)
+            h2.append(silu_blocks(accs, s1, b1_sb, f"h2_{half}"))
+        for half, columns in enumerate(halves):
+            accs = project(wf_blocks, h2[half], block_by_block=False)
+            for c in range(BLOCKS):
+                result = held.tile([P, N // 2], F32, name=f"result{half}_{c}")
+                if c % 2 == 0:
+                    nc.vector.tensor_scalar_add(result[:], accs[c][:], bo_sb[:, c : c + 1])
+                else:
+                    nc.scalar.activation(result[:], accs[c][:], IDENTITY, bias=bo_sb[:, c : c + 1])
                 nc.sync.dma_start(out_blocks[:, c, columns], result[:])
-            else:
-                nc.scalar.activation(result[:], accs[t][:], IDENTITY, bias=bo_sb[:, c : c + 1])
-                nc.scalar.dma_start(out_blocks[:, c, columns], result[:])

@@ -5,7 +5,6 @@ P = 128
 D, S, H, O, N = 128, 512, 512, 512, 256
 BLOCKS = H // P
 assert D == P and H == O
-WARM_MATMULS = 16
 
 FLOPS = 2 * N * (D * H + H * H + H * O)
 BYTES = 2 * (D * N + D * H + H * H + H * O) + 4 * (4 * H + O) + 2 * P * (N // 16) + 4 * O * N
@@ -25,16 +24,11 @@ def tile_hypernetfullyconnectedflexilayersizearch_kernel(
         tc.tile_pool(name="scratch", bufs=2) as scratch,
         tc.psum_pool(name="psum", bufs=8) as psum,
     ):
-        warm_src = held.tile([P, P], BF16, name="warm_src")
-        nc.gpsimd.memset(warm_src[:], 0.0)
         identity = held.tile([P, P], F32, name="identity")
         make_identity(nc, identity[:])
         minus_half = held.tile([P, BLOCKS], F32, name="minus_half")
         nc.vector.memset(minus_half[:], -0.5)
 
-        warm_acc = psum.tile([P, P], F32, name="warm_acc", tag="bank")
-        for i in range(WARM_MATMULS):
-            nc.tensor.matmul(warm_acc[:], warm_src[:], warm_src[:], start=True, stop=True)
         warm_silu = held.tile([P, 1], F32, name="warm_silu")
         nc.scalar.activation(warm_silu[:], minus_half[:, 0:1], SILU)
 

@@ -99,22 +99,23 @@ def tile_hypernetfullyconnectedflexilayersizearch_kernel(
                 nc.tensor.matmul(
                     accs[c][:], weight_blocks[kb][:, c, :], moving_blocks[kb], start=kb == 0, stop=kb == BLOCKS - 1
                 )
-            return accs
+            return [acc[:] for acc in accs]
 
         def silu_blocks(accs, scale, bias, name):
-            width = accs[0][:].shape[1]
+            width = accs[0].shape[1]
             hidden = [held.tile([P, width], BF16, name=f"{name}_{c}") for c in range(BLOCKS)]
             for c in range(BLOCKS):
                 nc.scalar.activation(
-                    hidden[c][:], accs[c][:], SILU, bias=bias[:, c : c + 1], scale=scale[:, c : c + 1]
+                    hidden[c][:], accs[c], SILU, bias=bias[:, c : c + 1], scale=scale[:, c : c + 1]
                 )
             return [h[:] for h in hidden]
 
         s0 = weight_norm_scale(v0_blocks, g0_sb, BLOCKS // 2, "s0")
         looked_up = table_sb[:].indirect(offsets[:])
-        picked = [psum.tile([P, N], F32, name=f"picked{c}", tag="bank") for c in range(BLOCKS)]
+        picked_pairs = [psum.tile([P, 2, N], F32, name=f"picked{pair}", tag="bank") for pair in range(BLOCKS // 2)]
+        picked = [picked_pairs[c // 2][:, c % 2, :] for c in range(BLOCKS)]
         for c in range(BLOCKS):
-            nc.tensor.matmul(picked[c][:], v0_blocks[0][:, c, :], looked_up, start=True, stop=True)
+            nc.tensor.matmul(picked[c], v0_blocks[0][:, c, :], looked_up, start=True, stop=True)
         h1 = silu_blocks(picked, s0, b0_sb, "h1")
 
         halves = [slice(0, N // 2), slice(N // 2, N)]
@@ -128,7 +129,7 @@ def tile_hypernetfullyconnectedflexilayersizearch_kernel(
             for c in range(BLOCKS):
                 result = held.tile([P, N // 2], F32, name=f"result{half}_{c}")
                 if c % 2 == 0:
-                    nc.vector.tensor_scalar_add(result[:], accs[c][:], bo_sb[:, c : c + 1])
+                    nc.vector.tensor_scalar_add(result[:], accs[c], bo_sb[:, c : c + 1])
                 else:
-                    nc.scalar.activation(result[:], accs[c][:], IDENTITY, bias=bo_sb[:, c : c + 1])
+                    nc.scalar.activation(result[:], accs[c], IDENTITY, bias=bo_sb[:, c : c + 1])
                 nc.sync.dma_start(out_blocks[:, c, columns], result[:])

@@ -26,7 +26,7 @@ def tile_hypernetfullyconnectedflexilayersizearch_kernel(
     ):
         identity = held.tile([P, P], F32, name="identity")
         make_identity(nc, identity[:])
-        minus_half = held.tile([P, BLOCKS], F32, name="minus_half")
+        minus_half = held.tile([P, BLOCKS // 2], F32, name="minus_half")
         nc.vector.memset(minus_half[:], -0.5)
 
         warm_silu = held.tile([P, 1], F32, name="warm_silu")
@@ -45,8 +45,10 @@ def tile_hypernetfullyconnectedflexilayersizearch_kernel(
                 queue.dma_start(columns[:], vector.rearrange("(c p) one -> p (c one)", c=BLOCKS))
             return columns
 
-        v1_sb = held.tile([P, BLOCKS, H], BF16, name="v1_sb")
-        nc.sync.dma_start(v1_sb[:], v1.rearrange("(kb p) m -> p kb m", kb=BLOCKS))
+        v1_rows = v1.rearrange("(kb p) m -> kb p m", kb=BLOCKS)
+        v1_sb = [held.tile([P, H], BF16, name=f"v1_sb{kb}") for kb in range(BLOCKS)]
+        for kb in range(BLOCKS):
+            nc.sync.dma_start(v1_sb[kb][:], v1_rows[kb])
         g0_sb = load_vector(nc.sync, g0, "g0_sb")
         b0_sb = load_vector(nc.sync, b0, "b0_sb")
         g1_sb = load_vector(nc.sync, g1, "g1_sb")
@@ -56,35 +58,31 @@ def tile_hypernetfullyconnectedflexilayersizearch_kernel(
         bo_sb = load_vector(nc.sync, bo, "bo_sb")
 
         v0_blocks = [v0_sb[:].rearrange("k (c p) -> k c p", c=BLOCKS)]
-        v1_view = v1_sb[:].rearrange("k kb (c p) -> k kb c p", c=BLOCKS)
-        v1_blocks = [v1_view[:, kb] for kb in range(BLOCKS)]
+        v1_blocks = [block[:].rearrange("k (c p) -> k c p", c=BLOCKS) for block in v1_sb]
         wf_view = wf_sb[:].rearrange("k kb (c p) -> k kb c p", c=BLOCKS)
         wf_blocks = [wf_view[:, kb] for kb in range(BLOCKS)]
         out_blocks = out.rearrange("(c p) j -> p c j", c=BLOCKS)
 
-        def weight_norm_scale(weight_blocks, gain, blocks_at_a_time, name):
+        def weight_norm_scale(weight_blocks, gain, products_in_a_bank, name):
             sum_squares = held.tile([P, BLOCKS], F32, name=name + "_sum_squares")
             inverse_norm = held.tile([P, BLOCKS], F32, name=name + "_inverse_norm")
             scale = held.tile([P, BLOCKS], F32, name=name)
             last = len(weight_blocks) - 1
-            pieces = [range(first, first + blocks_at_a_time) for first in range(0, BLOCKS, blocks_at_a_time)]
-            for piece in pieces:
-                gram = psum.tile([P, blocks_at_a_time, P], F32, name="gram", tag="bank")
-                for i, c in enumerate(piece):
-                    for kb, block in enumerate(weight_blocks):
-                        nc.tensor.matmul(
-                            gram[:, i, :], block[:, c, :], block[:, c, :], start=kb == 0, stop=kb == last
-                        )
-                for i, c in enumerate(piece):
-                    diagonal = scratch.tile([P, P], F32, name="diagonal")
-                    nc.vector.scalar_tensor_tensor(
-                        diagonal[:], gram[:, i, :], 1.0, identity[:], MULT, MULT, accum_out=sum_squares[:, c : c + 1]
-                    )
-            for piece in pieces:
-                columns = slice(piece[0], piece[0] + blocks_at_a_time)
-                nc.gpsimd.tensor_tensor(
-                    inverse_norm[:, columns], sum_squares[:, columns], minus_half[:, 0:blocks_at_a_time], POW
+            banks = [
+                psum.tile([P, products_in_a_bank, P], F32, name=f"gram{b}", tag="bank")
+                for b in range(BLOCKS // products_in_a_bank)
+            ]
+            grams = [banks[c // products_in_a_bank][:, c % products_in_a_bank, :] for c in range(BLOCKS)]
+            for kb, block in enumerate(weight_blocks):
+                for c in range(BLOCKS):
+                    nc.tensor.matmul(grams[c], block[:, c, :], block[:, c, :], start=kb == 0, stop=kb == last)
+            for c in range(BLOCKS):
+                diagonal = scratch.tile([P, P], F32, name="diagonal")
+                nc.vector.scalar_tensor_tensor(
+                    diagonal[:], grams[c], 1.0, identity[:], MULT, MULT, accum_out=sum_squares[:, c : c + 1]
                 )
+            for columns in (slice(0, BLOCKS // 2), slice(BLOCKS // 2, BLOCKS)):
+                nc.gpsimd.tensor_tensor(inverse_norm[:, columns], sum_squares[:, columns], minus_half[:], POW)
                 nc.vector.tensor_tensor(scale[:, columns], inverse_norm[:, columns], gain[:, columns], MULT)
             return scale
 
@@ -110,7 +108,7 @@ def tile_hypernetfullyconnectedflexilayersizearch_kernel(
                 )
             return [h[:] for h in hidden]
 
-        s0 = weight_norm_scale(v0_blocks, g0_sb, BLOCKS // 2, "s0")
+        s0 = weight_norm_scale(v0_blocks, g0_sb, 2, "s0")
         looked_up = table_sb[:].indirect(offsets[:])
         picked_pairs = [psum.tile([P, 2, N], F32, name=f"picked{pair}", tag="bank") for pair in range(BLOCKS // 2)]
         picked = [picked_pairs[c // 2][:, c % 2, :] for c in range(BLOCKS)]
@@ -119,7 +117,7 @@ def tile_hypernetfullyconnectedflexilayersizearch_kernel(
         h1 = silu_blocks(picked, s0, b0_sb, "h1")
 
         halves = [slice(0, N // 2), slice(N // 2, N)]
-        s1 = weight_norm_scale(v1_blocks, g1_sb, BLOCKS // 2, "s1")
+        s1 = weight_norm_scale(v1_blocks, g1_sb, 1, "s1")
         h2 = []
         for half, columns in enumerate(halves):
             accs = project(v1_blocks, [h[:, columns] for h in h1], block_by_block=half == 0)

@@ -34,10 +34,6 @@ def tile_hypernetfullyconnectedflexilayersizearch_kernel(
 
         v0_sb = held.tile([P, H], BF16, name="v0_sb")
         nc.sync.dma_start(v0_sb[:], v0)
-        table_sb = held.tile([P, S], BF16, name="table_sb")
-        nc.sync.dma_start(table_sb[:], table)
-        offsets = held.tile([P, N // 16], U16, name="offsets")
-        nc.sync.dma_start(offsets[:], offs)
 
         def load_vector(queue, vector, name):
             columns = held.tile([P, BLOCKS], F32, name=name)
@@ -49,6 +45,10 @@ def tile_hypernetfullyconnectedflexilayersizearch_kernel(
         v1_sb = [held.tile([P, H], BF16, name=f"v1_sb{kb}") for kb in range(BLOCKS)]
         for kb in range(BLOCKS):
             nc.sync.dma_start(v1_sb[kb][:], v1_rows[kb])
+        table_sb = held.tile([P, S], BF16, name="table_sb")
+        nc.sync.dma_start(table_sb[:], table)
+        offsets = held.tile([P, N // 16], U16, name="offsets")
+        nc.sync.dma_start(offsets[:], offs)
         g0_sb = load_vector(nc.sync, g0, "g0_sb")
         b0_sb = load_vector(nc.sync, b0, "b0_sb")
         g1_sb = load_vector(nc.sync, g1, "g1_sb")
@@ -109,6 +109,8 @@ def tile_hypernetfullyconnectedflexilayersizearch_kernel(
             return [h[:] for h in hidden]
 
         s0 = weight_norm_scale(v0_blocks, g0_sb, 2, "s0")
+        s1 = weight_norm_scale(v1_blocks, g1_sb, 1, "s1")
+
         looked_up = table_sb[:].indirect(offsets[:])
         picked_pairs = [psum.tile([P, 2, N], F32, name=f"picked{pair}", tag="bank") for pair in range(BLOCKS // 2)]
         picked = [picked_pairs[c // 2][:, c % 2, :] for c in range(BLOCKS)]
@@ -117,7 +119,6 @@ def tile_hypernetfullyconnectedflexilayersizearch_kernel(
         h1 = silu_blocks(picked, s0, b0_sb, "h1")
 
         halves = [slice(0, N // 2), slice(N // 2, N)]
-        s1 = weight_norm_scale(v1_blocks, g1_sb, 1, "s1")
         h2 = []
         for half, columns in enumerate(halves):
             accs = project(v1_blocks, [h[:, columns] for h in h1], block_by_block=half == 0)

@@ -9,6 +9,8 @@ assert D == P and H == O
 FLOPS = 2 * N * (D * H + H * H + H * O)
 BYTES = 2 * (D * N + D * H + H * H + H * O) + 4 * (4 * H + O) + 2 * P * (N // 16) + 4 * O * N
 
+WARM_UP = 12
+
 BF16, F32, U16 = mybir.dt.bfloat16, mybir.dt.float32, mybir.dt.uint16
 MULT, POW = mybir.AluOpType.mult, mybir.AluOpType.pow
 SILU = mybir.ActivationFunctionType.Silu
@@ -31,6 +33,12 @@ def tile_hypernetfullyconnectedflexilayersizearch_kernel(
 
         warm_silu = held.tile([P, 1], F32, name="warm_silu")
         nc.scalar.activation(warm_silu[:], minus_half[:, 0:1], SILU)
+
+        zeros = held.tile([P, P], BF16, name="zeros")
+        nc.vector.memset(zeros[:], 0.0)
+        unread = psum.tile([P, P], F32, name="unread", tag="bank")
+        for repeat in range(WARM_UP):
+            nc.tensor.matmul(unread[:], zeros[:], zeros[:], start=True, stop=True)
 
         v0_sb = held.tile([P, H], BF16, name="v0_sb")
         nc.sync.dma_start(v0_sb[:], v0)

@@ -9,7 +9,7 @@ assert D == P and H == O
 FLOPS = 2 * N * (D * H + H * H + H * O)
 BYTES = 2 * (D * N + D * H + H * H + H * O) + 4 * (4 * H + O) + 2 * P * (N // 16) + 4 * O * N
 
-WARM_UP = 12
+WARM_UP = 14
 
 BF16, F32, U16 = mybir.dt.bfloat16, mybir.dt.float32, mybir.dt.uint16
 MULT, POW = mybir.AluOpType.mult, mybir.AluOpType.pow
@@ -26,6 +26,8 @@ def tile_hypernetfullyconnectedflexilayersizearch_kernel(
         tc.tile_pool(name="scratch", bufs=2) as scratch,
         tc.psum_pool(name="psum", bufs=8) as psum,
     ):
+        zeros = held.tile([P, P], BF16, name="zeros")
+        nc.gpsimd.memset(zeros[:].bitcast(F32), 0.0)
         identity = held.tile([P, P], F32, name="identity")
         make_identity(nc, identity[:])
         minus_half = held.tile([P, BLOCKS // 2], F32, name="minus_half")
@@ -34,8 +36,6 @@ def tile_hypernetfullyconnectedflexilayersizearch_kernel(
         warm_silu = held.tile([P, 1], F32, name="warm_silu")
         nc.scalar.activation(warm_silu[:], minus_half[:, 0:1], SILU)
 
-        zeros = held.tile([P, P], BF16, name="zeros")
-        nc.vector.memset(zeros[:], 0.0)
         unread = psum.tile([P, P], F32, name="unread", tag="bank")
         for repeat in range(WARM_UP):
             nc.tensor.matmul(unread[:], zeros[:], zeros[:], start=True, stop=True)
@@ -124,12 +124,15 @@ def tile_hypernetfullyconnectedflexilayersizearch_kernel(
         picked = [picked_pairs[c // 2][:, c % 2, :] for c in range(BLOCKS)]
         for c in range(BLOCKS):
             nc.tensor.matmul(picked[c], v0_blocks[0][:, c, :], looked_up, start=True, stop=True)
-        h1 = silu_blocks(picked, s0, b0_sb, "h1")
 
         halves = [slice(0, N // 2), slice(N // 2, N)]
-        h2 = []
+        h1 = []
         for half, columns in enumerate(halves):
-            accs = project(v1_blocks, [h[:, columns] for h in h1], block_by_block=half == 0)
+            h1.append(silu_blocks([product[:, columns] for product in picked], s0, b0_sb, f"h1_{half}"))
+
+        h2 = []
+        for half in range(2):
+            accs = project(v1_blocks, h1[half], block_by_block=half == 0)
             h2.append(silu_blocks(accs, s1, b1_sb, f"h2_{half}"))
         for half, columns in enumerate(halves):
             accs = project(wf_blocks, h2[half], block_by_block=False)

@@ -43,13 +43,13 @@ def tile_hypernetfullyconnectedflexilayersizearch_kernel(
         v0_sb = held.tile([P, H], BF16, name="v0_sb")
         nc.sync.dma_start(v0_sb[:], v0)
 
-        def load_vector(queue, vector, name):
+        def load_vector(vector, order, name):
             columns = held.tile([P, BLOCKS], F32, name=name)
-            with nc.allow_non_contiguous_dma(reason="512 floats, one to a partition and block"):
-                queue.dma_start(columns[:], vector.rearrange("(c p) one -> p (c one)", c=BLOCKS))
+            with nc.allow_non_contiguous_dma(reason="512 floats, four to a partition"):
+                nc.sync.dma_start(columns[:], vector.rearrange(order, c=BLOCKS))
             return columns
 
-        v1_rows = v1.rearrange("(kb p) m -> kb p m", kb=BLOCKS)
+        v1_rows = v1.rearrange("(p kb) m -> kb p m", kb=BLOCKS)
         v1_sb = [held.tile([P, H], BF16, name=f"v1_sb{kb}") for kb in range(BLOCKS)]
         for kb in range(BLOCKS):
             nc.sync.dma_start(v1_sb[kb][:], v1_rows[kb])
@@ -57,15 +57,15 @@ def tile_hypernetfullyconnectedflexilayersizearch_kernel(
         nc.sync.dma_start(table_sb[:], table)
         offsets = held.tile([P, N // 16], U16, name="offsets")
         nc.sync.dma_start(offsets[:], offs)
-        g0_sb = load_vector(nc.sync, g0, "g0_sb")
-        b0_sb = load_vector(nc.sync, b0, "b0_sb")
-        g1_sb = load_vector(nc.sync, g1, "g1_sb")
-        b1_sb = load_vector(nc.sync, b1, "b1_sb")
+        g0_sb = load_vector(g0, "(p c) one -> p (c one)", "g0_sb")
+        b0_sb = load_vector(b0, "(p c) one -> p (c one)", "b0_sb")
+        g1_sb = load_vector(g1, "(c p) one -> p (c one)", "g1_sb")
+        b1_sb = load_vector(b1, "(c p) one -> p (c one)", "b1_sb")
         wf_sb = held.tile([P, BLOCKS, O], BF16, name="wf_sb")
         nc.sync.dma_start(wf_sb[:], wf.rearrange("(kb p) m -> p kb m", kb=BLOCKS))
-        bo_sb = load_vector(nc.sync, bo, "bo_sb")
+        bo_sb = load_vector(bo, "(c p) one -> p (c one)", "bo_sb")
 
-        v0_blocks = [v0_sb[:].rearrange("k (c p) -> k c p", c=BLOCKS)]
+        v0_blocks = [v0_sb[:].rearrange("k (p c) -> k c p", c=BLOCKS)]
         v1_blocks = [block[:].rearrange("k (c p) -> k c p", c=BLOCKS) for block in v1_sb]
         wf_view = wf_sb[:].rearrange("k kb (c p) -> k kb c p", c=BLOCKS)
         wf_blocks = [wf_view[:, kb] for kb in range(BLOCKS)]

@@ -9,7 +9,9 @@ assert D == P and H == O
 FLOPS = 2 * N * (D * H + H * H + H * O)
 BYTES = 2 * (D * N + D * H + H * H + H * O) + 4 * (4 * H + O) + 2 * P * (N // 16) + 4 * O * N
 
-WARM_UP = 14
+WARM_UP = 3
+BANK = 512
+COLUMN_TILE = 32
 
 BF16, F32, U16 = mybir.dt.bfloat16, mybir.dt.float32, mybir.dt.uint16
 MULT, POW = mybir.AluOpType.mult, mybir.AluOpType.pow
@@ -26,7 +28,7 @@ def tile_hypernetfullyconnectedflexilayersizearch_kernel(
         tc.tile_pool(name="scratch", bufs=2) as scratch,
         tc.psum_pool(name="psum", bufs=8) as psum,
     ):
-        zeros = held.tile([P, P], BF16, name="zeros")
+        zeros = held.tile([P, COLUMN_TILE], BF16, name="zeros")
         nc.gpsimd.memset(zeros[:].bitcast(F32), 0.0)
         identity = held.tile([P, P], F32, name="identity")
         make_identity(nc, identity[:])
@@ -36,9 +38,16 @@ def tile_hypernetfullyconnectedflexilayersizearch_kernel(
         warm_silu = held.tile([P, 1], F32, name="warm_silu")
         nc.scalar.activation(warm_silu[:], minus_half[:, 0:1], SILU)
 
-        unread = psum.tile([P, P], F32, name="unread", tag="bank")
+        unread = psum.tile([P, BANK], F32, name="unread", tag="bank")
         for repeat in range(WARM_UP):
-            nc.tensor.matmul(unread[:], zeros[:], zeros[:], start=True, stop=True)
+            for first in range(0, P, COLUMN_TILE):
+                nc.tensor.matmul(
+                    unread[first : first + COLUMN_TILE, :],
+                    zeros[:],
+                    zeros[:, 0:1].to_broadcast([P, BANK]),
+                    start=True,
+                    stop=True,
+                )
 
         v0_sb = held.tile([P, H], BF16, name="v0_sb")
         nc.sync.dma_start(v0_sb[:], v0)

import concourse.mybir as mybir
from concourse.masks import make_identity

P = 128
D, S, H, O, N = 128, 512, 512, 512, 256
BLOCKS = H // P
assert D == P and H == O

FLOPS = 2 * N * (D * H + H * H + H * O)
BYTES = 2 * (D * N + D * H + H * H + H * O) + 4 * (4 * H + O) + 2 * P * (N // 16) + 4 * O * N

WARM_UP = 3
BANK = 512
COLUMN_TILE = 32

BF16, F32, U16 = mybir.dt.bfloat16, mybir.dt.float32, mybir.dt.uint16
MULT, POW = mybir.AluOpType.mult, mybir.AluOpType.pow
SILU = mybir.ActivationFunctionType.Silu
IDENTITY = mybir.ActivationFunctionType.Identity


def tile_hypernetfullyconnectedflexilayersizearch_kernel(
    tc, table, v0, g0, b0, v1, g1, b1, wf, bo, offs, out
):
    nc = tc.nc
    with (
        tc.tile_pool(name="held", bufs=1) as held,
        tc.tile_pool(name="scratch", bufs=2) as scratch,
        tc.psum_pool(name="psum", bufs=8) as psum,
    ):
        zeros = held.tile([P, COLUMN_TILE], BF16, name="zeros")
        nc.gpsimd.memset(zeros[:].bitcast(F32), 0.0)
        identity = held.tile([P, P], F32, name="identity")
        make_identity(nc, identity[:])
        minus_half = held.tile([P, BLOCKS // 2], F32, name="minus_half")
        nc.vector.memset(minus_half[:], -0.5)

        warm_silu = held.tile([P, 1], F32, name="warm_silu")
        nc.scalar.activation(warm_silu[:], minus_half[:, 0:1], SILU)

        unread = psum.tile([P, BANK], F32, name="unread", tag="bank")
        for repeat in range(WARM_UP):
            for first in range(0, P, COLUMN_TILE):
                nc.tensor.matmul(
                    unread[first : first + COLUMN_TILE, :],
                    zeros[:],
                    zeros[:, 0:1].to_broadcast([P, BANK]),
                    start=True,
                    stop=True,
                )

        v0_sb = held.tile([P, H], BF16, name="v0_sb")
        nc.sync.dma_start(v0_sb[:], v0)

        def load_vector(vector, order, name):
            columns = held.tile([P, BLOCKS], F32, name=name)
            with nc.allow_non_contiguous_dma(reason="512 floats, four to a partition"):
                nc.sync.dma_start(columns[:], vector.rearrange(order, c=BLOCKS))
            return columns

        v1_rows = v1.rearrange("(p kb) m -> kb p m", kb=BLOCKS)
        v1_sb = [held.tile([P, H], BF16, name=f"v1_sb{kb}") for kb in range(BLOCKS)]
        for kb in range(BLOCKS):
            nc.sync.dma_start(v1_sb[kb][:], v1_rows[kb])
        table_sb = held.tile([P, S], BF16, name="table_sb")
        nc.sync.dma_start(table_sb[:], table)
        offsets = held.tile([P, N // 16], U16, name="offsets")
        nc.sync.dma_start(offsets[:], offs)
        g0_sb = load_vector(g0, "(p c) one -> p (c one)", "g0_sb")
        b0_sb = load_vector(b0, "(p c) one -> p (c one)", "b0_sb")
        g1_sb = load_vector(g1, "(c p) one -> p (c one)", "g1_sb")
        b1_sb = load_vector(b1, "(c p) one -> p (c one)", "b1_sb")
        wf_sb = held.tile([P, BLOCKS, O], BF16, name="wf_sb")
        nc.sync.dma_start(wf_sb[:], wf.rearrange("(kb p) m -> p kb m", kb=BLOCKS))
        bo_sb = load_vector(bo, "(c p) one -> p (c one)", "bo_sb")

        v0_blocks = [v0_sb[:].rearrange("k (p c) -> k c p", c=BLOCKS)]
        v1_blocks = [block[:].rearrange("k (c p) -> k c p", c=BLOCKS) for block in v1_sb]
        wf_view = wf_sb[:].rearrange("k kb (c p) -> k kb c p", c=BLOCKS)
        wf_blocks = [wf_view[:, kb] for kb in range(BLOCKS)]
        out_blocks = out.rearrange("(c p) j -> p c j", c=BLOCKS)

        def weight_norm_scale(weight_blocks, gain, products_in_a_bank, name):
            sum_squares = held.tile([P, BLOCKS], F32, name=name + "_sum_squares")
            inverse_norm = held.tile([P, BLOCKS], F32, name=name + "_inverse_norm")
            scale = held.tile([P, BLOCKS], F32, name=name)
            last = len(weight_blocks) - 1
            banks = [
                psum.tile([P, products_in_a_bank, P], F32, name=f"gram{b}", tag="bank")
                for b in range(BLOCKS // products_in_a_bank)
            ]
            grams = [banks[c // products_in_a_bank][:, c % products_in_a_bank, :] for c in range(BLOCKS)]
            for kb, block in enumerate(weight_blocks):
                for c in range(BLOCKS):
                    nc.tensor.matmul(grams[c], block[:, c, :], block[:, c, :], start=kb == 0, stop=kb == last)
            for c in range(BLOCKS):
                diagonal = scratch.tile([P, P], F32, name="diagonal")
                nc.vector.scalar_tensor_tensor(
                    diagonal[:], grams[c], 1.0, identity[:], MULT, MULT, accum_out=sum_squares[:, c : c + 1]
                )
            for columns in (slice(0, BLOCKS // 2), slice(BLOCKS // 2, BLOCKS)):
                nc.gpsimd.tensor_tensor(inverse_norm[:, columns], sum_squares[:, columns], minus_half[:], POW)
                nc.vector.tensor_tensor(scale[:, columns], inverse_norm[:, columns], gain[:, columns], MULT)
            return scale

        def project(weight_blocks, moving_blocks, block_by_block):
            width = moving_blocks[0].shape[1]
            accs = [psum.tile([P, width], F32, name=f"acc{c}", tag="bank") for c in range(BLOCKS)]
            if block_by_block:
                order = [(c, kb) for kb in range(BLOCKS) for c in range(BLOCKS)]
            else:
                order = [(c, kb) for c in range(BLOCKS) for kb in range(BLOCKS)]
            for c, kb in order:
                nc.tensor.matmul(
                    accs[c][:], weight_blocks[kb][:, c, :], moving_blocks[kb], start=kb == 0, stop=kb == BLOCKS - 1
                )
            return [acc[:] for acc in accs]

        def silu_blocks(accs, scale, bias, name):
            width = accs[0].shape[1]
            hidden = [held.tile([P, width], BF16, name=f"{name}_{c}") for c in range(BLOCKS)]
            for c in range(BLOCKS):
                nc.scalar.activation(
                    hidden[c][:], accs[c], SILU, bias=bias[:, c : c + 1], scale=scale[:, c : c + 1]
                )
            return [h[:] for h in hidden]

        s0 = weight_norm_scale(v0_blocks, g0_sb, 2, "s0")
        s1 = weight_norm_scale(v1_blocks, g1_sb, 1, "s1")

        looked_up = table_sb[:].indirect(offsets[:])
        picked_pairs = [psum.tile([P, 2, N], F32, name=f"picked{pair}", tag="bank") for pair in range(BLOCKS // 2)]
        picked = [picked_pairs[c // 2][:, c % 2, :] for c in range(BLOCKS)]
        for c in range(BLOCKS):
            nc.tensor.matmul(picked[c], v0_blocks[0][:, c, :], looked_up, start=True, stop=True)

        halves = [slice(0, N // 2), slice(N // 2, N)]
        h1 = []
        for half, columns in enumerate(halves):
            h1.append(silu_blocks([product[:, columns] for product in picked], s0, b0_sb, f"h1_{half}"))

        h2 = []
        for half in range(2):
            accs = project(v1_blocks, h1[half], block_by_block=half == 0)
            h2.append(silu_blocks(accs, s1, b1_sb, f"h2_{half}"))
        for half, columns in enumerate(halves):
            accs = project(wf_blocks, h2[half], block_by_block=False)
            for c in range(BLOCKS):
                result = held.tile([P, N // 2], F32, name=f"result{half}_{c}")
                if c % 2 == 0:
                    nc.vector.tensor_scalar_add(result[:], accs[c], bo_sb[:, c : c + 1])
                else:
                    nc.scalar.activation(result[:], accs[c], IDENTITY, bias=bo_sb[:, c : c + 1])
                nc.sync.dma_start(out_blocks[:, c, columns], result[:])
